import numpy as np
import ml_dtypes


def mxq(x, axis, fmt="e4m3"):
    dtype, down = {"e4m3": (ml_dtypes.float8_e4m3fn, 7), "e5m2": (ml_dtypes.float8_e5m2, 14)}[fmt]
    v = np.moveaxis(np.asarray(x, np.float32).astype(ml_dtypes.bfloat16).astype(np.float64), axis, -1)
    blocks = v.reshape(v.shape[:-1] + (-1, 32))
    amax = np.abs(blocks).max(-1, keepdims=True)
    byte = np.maximum(np.where(amax > 0, np.frexp(amax)[1] - 1 + 127, 0) - down, 1)
    scale = np.exp2(byte - 127.0)
    codes = (blocks / scale).astype(np.float32).astype(dtype).astype(np.float64)
    return np.moveaxis((codes * scale).reshape(v.shape), -1, axis)


WIDE = False


def mx_kscale(k):
    if not WIDE:
        return np.ones(k)
    levels = np.array([10, -10, 5, -5, 0])
    if k % 512:
        return np.exp2(np.random.permutation(np.resize(levels, k // 32))).repeat(32)
    a = np.empty((k // 512, 16))
    for p in range(k // 512):
        a[p, :8] = np.random.permutation(np.resize(levels, 8))
        for g in range(8):
            far = levels[np.abs(levels - a[p, g]) >= 10]
            a[p, g + 8] = far[np.random.randint(len(far))]
    return np.exp2(a.ravel()).repeat(32)


BF16 = ml_dtypes.bfloat16


def bf(x):
    return np.asarray(x, np.float32).astype(BF16)


def f64(x):
    return np.asarray(x).astype(np.float64)


B, D_IN, D_H = 512, 1024, 1024


def sigmoid(v):
    return 1.0 / (1.0 + np.exp(-v))


def setup_inputs():
    s, t = mx_kscale(D_IN), mx_kscale(D_H)
    fg = np.exp(0.75 * np.random.standard_normal((B, D_H)))
    ig = np.exp(0.75 * np.random.standard_normal((B, D_H)))
    c = fg * np.random.standard_normal((B, D_H)) + ig * np.tanh(0.75 * np.random.standard_normal((B, D_H)))
    n = fg * np.random.uniform(size=(B, D_H)) + ig
    return {"x": bf(np.random.standard_normal((B, D_IN)) * s),
            "h_prev": bf(np.random.standard_normal((B, D_H)) * t),
            "c": bf(c),
            "n": bf(n),
            "W_o": bf(np.random.standard_normal((D_IN, D_H)) * 0.5 / np.sqrt(D_IN) / s[:, None]),
            "b_o": bf(np.random.standard_normal(D_H) * 0.3),
            "U_o": bf(np.random.standard_normal((D_H, D_H)) * 0.5 / np.sqrt(D_H) / t[:, None])}


def reference(x, h_prev, c, n, W_o, b_o, U_o):
    o = sigmoid((mxq(f64(x), 1, "e4m3") @ mxq(f64(W_o), 0, "e4m3")) + f64(b_o) + (mxq(f64(h_prev), 1, "e4m3") @ mxq(f64(U_o), 0, "e4m3")))
    return o * (f64(c) / (f64(n) + 1e-6))

@@ -1,0 +1,193 @@
+from contextlib import ExitStack
+
+import concourse.masks as masks
+import concourse.mybir as mybir
+
+F32 = mybir.dt.float32
+BF16 = mybir.dt.bfloat16
+U32 = mybir.dt.uint32
+U8 = mybir.dt.uint8
+FP8X4 = mybir.dt.float8_e4m3fn_x4
+ACT = mybir.ActivationFunctionType
+ALU = mybir.AluOpType
+
+P = 128
+BATCH = 512
+FEAT = 1024
+NB = BATCH // P
+NJ = FEAT // P
+K_PASS = 4 * P
+PASSES = 2 * FEAT // K_PASS
+EPS = 1e-6
+
+SCALAR_COLS = (0, 0, 256, 512)
+
+FLOPS = 2 * BATCH * FEAT * FEAT * 2
+
+
+def tile_slstmcell_pb_kernel(tc, x, h_prev, c, n, W_o, b_o, U_o, out):
+    nc = tc.nc
+    with ExitStack() as ctx:
+        keep = ctx.enter_context(tc.tile_pool(name="keep", bufs=1))
+        psum = ctx.enter_context(tc.psum_pool(name="psum", bufs=1))
+
+        ident = keep.tile([P, P], F32, name="ident")
+        masks.make_identity(nc, ident[:])
+        eps2 = keep.tile([P, 1], F32, name="eps2")
+        nc.vector.memset(eps2[:], 2.0 * EPS)
+        bias_rows = keep.tile([P, P], BF16, name="bias_rows")
+        nc.vector.memset(bias_rows[:], 0.0)
+
+        acts = [x, h_prev]
+        weights = [W_o, U_o]
+        act_sb = [keep.tile([P, NB, FEAT], BF16, name="act_sb%d" % o) for o in range(2)]
+        n_sb = keep.tile([P, NB, FEAT], BF16, name="n_sb")
+        c_sb = keep.tile([P, NB, FEAT], BF16, name="c_sb")
+        w_rows = [keep.tile([P, 4, FEAT], BF16, name="w_rows%d" % g) for g in range(PASSES)]
+        w_words = [keep.tile([P, FEAT, 4], BF16, name="w_words%d" % g, align_bytes=64) for g in range(PASSES)]
+        w_codes = keep.tile([P, PASSES, FEAT], U32, name="w_codes", align_bytes=64)
+        w_scales = keep.tile([P, PASSES, FEAT], U8, name="w_scales", align_bytes=64)
+        a_words = [keep.tile([P, BATCH * 4], BF16, name="a_words%d" % g, align_bytes=64) for g in range(PASSES)]
+        a_codes = keep.tile([P, PASSES, BATCH], U32, name="a_codes", align_bytes=64)
+        a_scales = keep.tile([P, PASSES, BATCH], U8, name="a_scales", align_bytes=64)
+        ratio = keep.tile([P, NB, FEAT], F32, name="ratio")
+        gate_t = [keep.tile([P, BATCH], F32, name="gate_t%d" % j) for j in range(NJ)]
+        h_sb = keep.tile([P, NB, FEAT], F32, name="h_sb")
+        bias_f32 = keep.tile([P, P], F32, name="bias_f32")
+        bias_half = keep.tile([P, NJ], F32, name="bias_half")
+        bias_ps = psum.tile([P, P], F32, name="bias_ps", tag="bank7")
+        flipped = {}
+        acc = {}
+        gate = {}
+
+        def by_partition(rows):
+            return rows.rearrange("(p b) d -> p b d", b=NB)
+
+        def load_rows(dst, src, lo, hi):
+            nc.sync.dma_start(out=dst[:, lo:hi, :], in_=by_partition(src)[:, lo:hi, :])
+
+        def load_weights(g):
+            rows = weights[g // 2][K_PASS * (g % 2) : K_PASS * (g % 2 + 1), :]
+            nc.sync.dma_start(out=w_rows[g][:], in_=rows.rearrange("(p t) w -> p t w", t=4))
+
+        def interleave(g):
+            cut = FEAT - SCALAR_COLS[g]
+            for copy, a, b in ((nc.vector.tensor_copy, 0, cut), (nc.scalar.copy, cut, FEAT)):
+                if b > a:
+                    copy(
+                        out=w_words[g][:, a:b, :].rearrange("p (w i) t -> p w t i", i=4),
+                        in_=w_rows[g][:, :, a:b].rearrange("p t (w i) -> p w t i", i=4),
+                    )
+
+        def quantise_weights(g):
+            nc.vector.quantize_mx(
+                out=w_codes[:, g, :].bitcast(FP8X4),
+                scales=w_scales[:, g, :],
+                in_=w_words[g][:].rearrange("p w t -> p (w t)"),
+            )
+
+        def flip_acts(o):
+            for pair in range(NB // 2):
+                for g in (2 * o, 2 * o + 1):
+                    bank = psum.tile([P, 2, 2 * P], F32, name="flipped%d_%d" % (g, pair), tag="bank%d" % (2 * g + pair))
+                    flipped[(g, pair)] = bank
+                    for u in range(2):
+                        for i in range(2):
+                            words = act_sb[o][:, 2 * pair + i, :].bitcast(F32)
+                            first = (K_PASS // 2) * (g % 2)
+                            nc.tensor.transpose(
+                                bank[:, u, i * P : (i + 1) * P], words[:, first + u : first + K_PASS // 2 : 2], ident[:]
+                            )
+            for pair in range(NB // 2):
+                for g in (2 * o, 2 * o + 1):
+                    dst = a_words[g][:].bitcast(F32).rearrange("p (r u) -> p r u", u=2)
+                    nc.scalar.copy(
+                        out=dst[:, 2 * P * pair : 2 * P * (pair + 1), :],
+                        in_=flipped[(g, pair)][:].rearrange("p u r -> p r u"),
+                    )
+
+        def quantise_acts(g):
+            nc.vector.quantize_mx(out=a_codes[:, g, :].bitcast(FP8X4), scales=a_scales[:, g, :], in_=a_words[g][:])
+
+        def spread_bias():
+            nc.vector.tensor_copy(out=bias_f32[:], in_=bias_rows[:])
+            nc.tensor.transpose(bias_ps[:], bias_f32[:], ident[:])
+            nc.vector.tensor_scalar_mul(out=bias_half[:], in0=bias_ps[:, 0:NJ], scalar1=0.5)
+
+        def log_n(b):
+            nc.scalar.activation(out=ratio[:, b, :], in_=n_sb[:, b, :], func=ACT.Ln, bias=eps2[:, 0:1], scale=2.0)
+
+        def reciprocal(b):
+            nc.scalar.activation(out=ratio[:, b, :], in_=ratio[:, b, :], func=ACT.Exp, scale=-1.0)
+
+        def times_c(b):
+            nc.vector.tensor_tensor(out=ratio[:, b, :], in0=c_sb[:, b, :], in1=ratio[:, b, :], op=ALU.mult)
+
+        def matmul_pass(g):
+            for j in range(NJ):
+                if g == 0:
+                    acc[j] = psum.tile([P, BATCH], F32, name="acc%d" % j, tag="bank%d" % j)
+                nc.tensor.matmul_mx(
+                    out=acc[j][:],
+                    lhsT=w_codes[:, g, j * P : (j + 1) * P].bitcast(FP8X4),
+                    lhsT_scale=w_scales[:, g, j * P : (j + 1) * P],
+                    rhs=a_codes[:, g, :].bitcast(FP8X4),
+                    rhs_scale=a_scales[:, g, :],
+                    start=(g == 0),
+                    stop=(g == PASSES - 1),
+                )
+
+        def finish(j):
+            cols = slice(j * P, (j + 1) * P)
+            nc.scalar.activation(out=gate_t[j][:], in_=acc[j][:], func=ACT.Tanh, bias=bias_half[:, j : j + 1], scale=0.5)
+            gate[j] = psum.tile([P, NB, P], F32, name="gate%d" % j, tag="bank%d" % j)
+            for b in range(NB):
+                nc.tensor.transpose(gate[j][:, b, :], gate_t[j][:, b * P : (b + 1) * P], ident[:])
+            nc.vector.scalar_tensor_tensor(
+                out=h_sb[:, :, cols], in0=gate[j][:], scalar=1.0, in1=ratio[:, :, cols], op0=ALU.add, op1=ALU.mult
+            )
+
+        def store(j0, j1):
+            cols = slice(j0 * P, j1 * P)
+            nc.sync.dma_start(out=by_partition(out)[:, :, cols], in_=h_sb[:, :, cols])
+
+        with tc.manual_schedule():
+            load_rows(n_sb, n, 0, 1)
+            load_weights(0)
+            nc.sync.dma_start(out=bias_rows[0:NJ, :], in_=b_o.rearrange("(j p) -> j p", p=P))
+            for b in range(1, NB):
+                load_rows(n_sb, n, b, b + 1)
+            load_weights(1)
+            load_rows(act_sb[0], x, 0, 2)
+            load_rows(act_sb[0], x, 2, 4)
+            load_weights(2)
+            load_rows(act_sb[1], h_prev, 0, 2)
+            load_rows(act_sb[1], h_prev, 2, 4)
+            load_weights(3)
+            load_rows(c_sb, c, 0, 2)
+            load_rows(c_sb, c, 2, 4)
+
+            for b in range(NB):
+                log_n(b)
+            interleave(0)
+            quantise_weights(0)
+            spread_bias()
+            interleave(1)
+            reciprocal(0)
+            quantise_weights(1)
+            for o in range(2):
+                flip_acts(o)
+                interleave(2 + o)
+                quantise_acts(2 * o)
+                quantise_acts(2 * o + 1)
+                quantise_weights(2 + o)
+            for b in range(1, NB):
+                reciprocal(b)
+            for b in range(NB):
+                times_c(b)
+            for g in range(PASSES):
+                matmul_pass(g)
+            for j in range(NJ):
+                finish(j)
+                if j % 2 == 1:
+                    store(j - 1, j + 1)

@@ -53,6 +53,7 @@ def tile_slstmcell_pb_kernel(tc, x, h_prev, c, n, W_o, b_o, U_o, out):
         ratio = keep.tile([P, NB, FEAT], F32, name="ratio")
         gate_t = [keep.tile([P, BATCH], F32, name="gate_t%d" % j) for j in range(NJ)]
         h_sb = keep.tile([P, NB, FEAT], F32, name="h_sb")
+        warm = keep.tile([P, 1], F32, name="warm")
         bias_f32 = keep.tile([P, P], F32, name="bias_f32")
         bias_half = keep.tile([P, NJ], F32, name="bias_half")
         bias_ps = psum.tile([P, P], F32, name="bias_ps", tag="bank7")
@@ -114,11 +115,13 @@ def tile_slstmcell_pb_kernel(tc, x, h_prev, c, n, W_o, b_o, U_o, out):
             nc.tensor.transpose(bias_ps[:], bias_f32[:], ident[:])
             nc.vector.tensor_scalar_mul(out=bias_half[:], in0=bias_ps[:, 0:NJ], scalar1=0.5)
 
-        def log_n(b):
-            nc.scalar.activation(out=ratio[:, b, :], in_=n_sb[:, b, :], func=ACT.Ln, bias=eps2[:, 0:1], scale=2.0)
+        def inverse_root(b):
+            nc.scalar.activation(
+                out=ratio[:, b, :], in_=n_sb[:, b, :], func=ACT.Abs_reciprocal_sqrt, bias=eps2[:, 0:1], scale=2.0
+            )
 
         def reciprocal(b):
-            nc.scalar.activation(out=ratio[:, b, :], in_=ratio[:, b, :], func=ACT.Exp, scale=-1.0)
+            nc.scalar.activation(out=ratio[:, b, :], in_=ratio[:, b, :], func=ACT.Square)
 
         def times_c(b):
             nc.vector.tensor_tensor(out=ratio[:, b, :], in0=c_sb[:, b, :], in1=ratio[:, b, :], op=ALU.mult)
@@ -152,11 +155,10 @@ def tile_slstmcell_pb_kernel(tc, x, h_prev, c, n, W_o, b_o, U_o, out):
             nc.sync.dma_start(out=by_partition(out)[:, :, cols], in_=h_sb[:, :, cols])
 
         with tc.manual_schedule():
-            load_rows(n_sb, n, 0, 1)
             load_weights(0)
+            load_rows(n_sb, n, 0, 1)
             nc.sync.dma_start(out=bias_rows[0:NJ, :], in_=b_o.rearrange("(j p) -> j p", p=P))
-            for b in range(1, NB):
-                load_rows(n_sb, n, b, b + 1)
+            load_rows(n_sb, n, 1, NB)
             load_weights(1)
             load_rows(act_sb[0], x, 0, 2)
             load_rows(act_sb[0], x, 2, 4)
@@ -167,13 +169,16 @@ def tile_slstmcell_pb_kernel(tc, x, h_prev, c, n, W_o, b_o, U_o, out):
             load_rows(c_sb, c, 0, 2)
             load_rows(c_sb, c, 2, 4)
 
-            for b in range(NB):
-                log_n(b)
+            nc.scalar.activation(out=warm[:], in_=eps2[:], func=ACT.Abs_reciprocal_sqrt)
+            inverse_root(0)
+            reciprocal(0)
+            for b in range(1, NB):
+                inverse_root(b)
+            reciprocal(1)
             interleave(0)
             quantise_weights(0)
             spread_bias()
             interleave(1)
-            reciprocal(0)
             quantise_weights(1)
             for o in range(2):
                 flip_acts(o)
@@ -181,7 +186,7 @@ def tile_slstmcell_pb_kernel(tc, x, h_prev, c, n, W_o, b_o, U_o, out):
                 quantise_acts(2 * o)
                 quantise_acts(2 * o + 1)
                 quantise_weights(2 + o)
-            for b in range(1, NB):
+            for b in range(2, NB):
                 reciprocal(b)
             for b in range(NB):
                 times_c(b)

@@ -20,7 +20,8 @@ K_PASS = 4 * P
 PASSES = 2 * FEAT // K_PASS
 EPS = 1e-6
 
-SCALAR_COLS = (0, 0, 256, 512)
+SCALAR_COLS = 512
+VECTOR_TILES = 5
 
 FLOPS = 2 * BATCH * FEAT * FEAT * 2
 
@@ -50,7 +51,10 @@ def tile_slstmcell_pb_kernel(tc, x, h_prev, c, n, W_o, b_o, U_o, out):
         a_words = [keep.tile([P, BATCH * 4], BF16, name="a_words%d" % g, align_bytes=64) for g in range(PASSES)]
         a_codes = keep.tile([P, PASSES, BATCH], U32, name="a_codes", align_bytes=64)
         a_scales = keep.tile([P, PASSES, BATCH], U8, name="a_scales", align_bytes=64)
-        ratio = keep.tile([P, NB, FEAT], F32, name="ratio")
+        inverse = keep.tile([P, NB, FEAT], F32, name="inverse")
+        ratio_vector = keep.tile([P, NB, VECTOR_TILES * P], F32, name="ratio_vector")
+        ratio_gpsimd = [keep.tile([P, NB, P], F32, name="ratio_gpsimd%d" % j) for j in range(VECTOR_TILES, NJ)]
+        mark = keep.tile([P, 1], F32, name="mark")
         gate_t = [keep.tile([P, BATCH], F32, name="gate_t%d" % j) for j in range(NJ)]
         h_sb = keep.tile([P, NB, FEAT], F32, name="h_sb")
         warm = keep.tile([P, 1], F32, name="warm")
@@ -71,14 +75,11 @@ def tile_slstmcell_pb_kernel(tc, x, h_prev, c, n, W_o, b_o, U_o, out):
             rows = weights[g // 2][K_PASS * (g % 2) : K_PASS * (g % 2 + 1), :]
             nc.sync.dma_start(out=w_rows[g][:], in_=rows.rearrange("(p t) w -> p t w", t=4))
 
-        def interleave(g):
-            cut = FEAT - SCALAR_COLS[g]
-            for copy, a, b in ((nc.vector.tensor_copy, 0, cut), (nc.scalar.copy, cut, FEAT)):
-                if b > a:
-                    copy(
-                        out=w_words[g][:, a:b, :].rearrange("p (w i) t -> p w t i", i=4),
-                        in_=w_rows[g][:, :, a:b].rearrange("p t (w i) -> p w t i", i=4),
-                    )
+        def interleave(copy, g, lo, hi):
+            copy(
+                out=w_words[g][:, lo:hi, :].rearrange("p (w i) t -> p w t i", i=4),
+                in_=w_rows[g][:, :, lo:hi].rearrange("p t (w i) -> p w t i", i=4),
+            )
 
         def quantise_weights(g):
             nc.vector.quantize_mx(
@@ -99,8 +100,8 @@ def tile_slstmcell_pb_kernel(tc, x, h_prev, c, n, W_o, b_o, U_o, out):
                             nc.tensor.transpose(
                                 bank[:, u, i * P : (i + 1) * P], words[:, first + u : first + K_PASS // 2 : 2], ident[:]
                             )
-            for pair in range(NB // 2):
-                for g in (2 * o, 2 * o + 1):
+            for g in (2 * o, 2 * o + 1):
+                for pair in range(NB // 2):
                     dst = a_words[g][:].bitcast(F32).rearrange("p (r u) -> p r u", u=2)
                     nc.scalar.copy(
                         out=dst[:, 2 * P * pair : 2 * P * (pair + 1), :],
@@ -110,21 +111,33 @@ def tile_slstmcell_pb_kernel(tc, x, h_prev, c, n, W_o, b_o, U_o, out):
         def quantise_acts(g):
             nc.vector.quantize_mx(out=a_codes[:, g, :].bitcast(FP8X4), scales=a_scales[:, g, :], in_=a_words[g][:])
 
-        def spread_bias():
+        def flip_bias():
             nc.vector.tensor_copy(out=bias_f32[:], in_=bias_rows[:])
             nc.tensor.transpose(bias_ps[:], bias_f32[:], ident[:])
+
+        def halve_bias():
             nc.vector.tensor_scalar_mul(out=bias_half[:], in0=bias_ps[:, 0:NJ], scalar1=0.5)
 
-        def inverse_root(b):
+        def half_reciprocal(b):
+            row = inverse[:, b, :]
             nc.scalar.activation(
-                out=ratio[:, b, :], in_=n_sb[:, b, :], func=ACT.Abs_reciprocal_sqrt, bias=eps2[:, 0:1], scale=2.0
+                out=row, in_=n_sb[:, b, :], func=ACT.Abs_reciprocal_sqrt, bias=eps2[:, 0:1], scale=2.0
+            )
+            nc.scalar.activation(out=row, in_=row, func=ACT.Square)
+
+        def vector_ratio(b):
+            cols = slice(0, VECTOR_TILES * P)
+            nc.vector.tensor_tensor(
+                out=ratio_vector[:, b, :], in0=c_sb[:, b, cols], in1=inverse[:, b, cols], op=ALU.mult
             )
 
-        def reciprocal(b):
-            nc.scalar.activation(out=ratio[:, b, :], in_=ratio[:, b, :], func=ACT.Square)
-
-        def times_c(b):
-            nc.vector.tensor_tensor(out=ratio[:, b, :], in0=c_sb[:, b, :], in1=ratio[:, b, :], op=ALU.mult)
+        def gpsimd_ratios():
+            nc.gpsimd.tensor_copy(out=mark[:], in_=ratio_vector[:, NB - 1, VECTOR_TILES * P - 1 : VECTOR_TILES * P])
+            for j in range(VECTOR_TILES, NJ):
+                cols = slice(j * P, (j + 1) * P)
+                nc.gpsimd.tensor_tensor(
+                    out=ratio_gpsimd[j - VECTOR_TILES][:], in0=c_sb[:, :, cols], in1=inverse[:, :, cols], op=ALU.mult
+                )
 
         def matmul_pass(g):
             for j in range(NJ):
@@ -140,14 +153,22 @@ def tile_slstmcell_pb_kernel(tc, x, h_prev, c, n, W_o, b_o, U_o, out):
                     stop=(g == PASSES - 1),
                 )
 
-        def finish(j):
-            cols = slice(j * P, (j + 1) * P)
+        def gate_of(j):
             nc.scalar.activation(out=gate_t[j][:], in_=acc[j][:], func=ACT.Tanh, bias=bias_half[:, j : j + 1], scale=0.5)
+
+        def turn_gate(j):
             gate[j] = psum.tile([P, NB, P], F32, name="gate%d" % j, tag="bank%d" % j)
             for b in range(NB):
                 nc.tensor.transpose(gate[j][:, b, :], gate_t[j][:, b * P : (b + 1) * P], ident[:])
+
+        def product(j):
+            cols = slice(j * P, (j + 1) * P)
+            if j < VECTOR_TILES:
+                ratio = ratio_vector[:, :, cols]
+            else:
+                ratio = ratio_gpsimd[j - VECTOR_TILES][:]
             nc.vector.scalar_tensor_tensor(
-                out=h_sb[:, :, cols], in0=gate[j][:], scalar=1.0, in1=ratio[:, :, cols], op0=ALU.add, op1=ALU.mult
+                out=h_sb[:, :, cols], in0=gate[j][:], scalar=1.0, in1=ratio, op0=ALU.add, op1=ALU.mult
             )
 
         def store(j0, j1):
@@ -156,43 +177,50 @@ def tile_slstmcell_pb_kernel(tc, x, h_prev, c, n, W_o, b_o, U_o, out):
 
         with tc.manual_schedule():
             load_weights(0)
-            load_rows(n_sb, n, 0, 1)
+            load_rows(n_sb, n, 0, 2)
             nc.sync.dma_start(out=bias_rows[0:NJ, :], in_=b_o.rearrange("(j p) -> j p", p=P))
-            load_rows(n_sb, n, 1, NB)
             load_weights(1)
             load_rows(act_sb[0], x, 0, 2)
             load_rows(act_sb[0], x, 2, 4)
-            load_weights(2)
             load_rows(act_sb[1], h_prev, 0, 2)
             load_rows(act_sb[1], h_prev, 2, 4)
+            load_weights(2)
+            load_rows(n_sb, n, 2, 3)
             load_weights(3)
+            load_rows(n_sb, n, 3, 4)
             load_rows(c_sb, c, 0, 2)
             load_rows(c_sb, c, 2, 4)
 
             nc.scalar.activation(out=warm[:], in_=eps2[:], func=ACT.Abs_reciprocal_sqrt)
-            inverse_root(0)
-            reciprocal(0)
-            for b in range(1, NB):
-                inverse_root(b)
-            reciprocal(1)
-            interleave(0)
+            half_reciprocal(0)
+            half_reciprocal(1)
+            interleave(nc.vector.tensor_copy, 0, 0, FEAT)
+            flip_bias()
             quantise_weights(0)
-            spread_bias()
-            interleave(1)
+            interleave(nc.vector.tensor_copy, 1, 0, FEAT)
+            halve_bias()
             quantise_weights(1)
-            for o in range(2):
-                flip_acts(o)
-                interleave(2 + o)
-                quantise_acts(2 * o)
-                quantise_acts(2 * o + 1)
-                quantise_weights(2 + o)
-            for b in range(2, NB):
-                reciprocal(b)
+            flip_acts(0)
+            quantise_acts(0)
+            quantise_acts(1)
+            interleave(nc.vector.tensor_copy, 2, 0, FEAT)
+            flip_acts(1)
+            half_reciprocal(2)
+            quantise_weights(2)
+            interleave(nc.vector.tensor_copy, 3, 0, FEAT - SCALAR_COLS)
+            interleave(nc.scalar.copy, 3, FEAT - SCALAR_COLS, FEAT)
+            quantise_acts(2)
+            quantise_acts(3)
+            quantise_weights(3)
+            half_reciprocal(3)
             for b in range(NB):
-                times_c(b)
+                vector_ratio(b)
+            gpsimd_ratios()
             for g in range(PASSES):
                 matmul_pass(g)
             for j in range(NJ):
-                finish(j)
+                gate_of(j)
+                turn_gate(j)
+                product(j)
                 if j % 2 == 1:
                     store(j - 1, j + 1)

@@ -20,7 +20,7 @@ K_PASS = 4 * P
 PASSES = 2 * FEAT // K_PASS
 EPS = 1e-6
 
-SCALAR_COLS = 512
+SPLIT = 3 * FEAT // 4
 VECTOR_TILES = 5
 
 FLOPS = 2 * BATCH * FEAT * FEAT * 2
@@ -88,25 +88,24 @@ def tile_slstmcell_pb_kernel(tc, x, h_prev, c, n, W_o, b_o, U_o, out):
                 in_=w_words[g][:].rearrange("p w t -> p (w t)"),
             )
 
-        def flip_acts(o):
-            for pair in range(NB // 2):
-                for g in (2 * o, 2 * o + 1):
-                    bank = psum.tile([P, 2, 2 * P], F32, name="flipped%d_%d" % (g, pair), tag="bank%d" % (2 * g + pair))
-                    flipped[(g, pair)] = bank
-                    for u in range(2):
-                        for i in range(2):
-                            words = act_sb[o][:, 2 * pair + i, :].bitcast(F32)
-                            first = (K_PASS // 2) * (g % 2)
-                            nc.tensor.transpose(
-                                bank[:, u, i * P : (i + 1) * P], words[:, first + u : first + K_PASS // 2 : 2], ident[:]
-                            )
+        def flip_acts(o, pair):
             for g in (2 * o, 2 * o + 1):
-                for pair in range(NB // 2):
-                    dst = a_words[g][:].bitcast(F32).rearrange("p (r u) -> p r u", u=2)
-                    nc.scalar.copy(
-                        out=dst[:, 2 * P * pair : 2 * P * (pair + 1), :],
-                        in_=flipped[(g, pair)][:].rearrange("p u r -> p r u"),
-                    )
+                bank = psum.tile([P, 2, 2 * P], F32, name="flipped%d_%d" % (g, pair), tag="bank%d" % (2 * g + pair))
+                flipped[(g, pair)] = bank
+                for u in range(2):
+                    for i in range(2):
+                        words = act_sb[o][:, 2 * pair + i, :].bitcast(F32)
+                        first = (K_PASS // 2) * (g % 2)
+                        nc.tensor.transpose(
+                            bank[:, u, i * P : (i + 1) * P], words[:, first + u : first + K_PASS // 2 : 2], ident[:]
+                        )
+
+        def unload_acts(copy, g, pair):
+            dst = a_words[g][:].bitcast(F32).rearrange("p (r u) -> p r u", u=2)
+            copy(
+                out=dst[:, 2 * P * pair : 2 * P * (pair + 1), :],
+                in_=flipped[(g, pair)][:].rearrange("p u r -> p r u"),
+            )
 
         def quantise_acts(g):
             nc.vector.quantize_mx(out=a_codes[:, g, :].bitcast(FP8X4), scales=a_scales[:, g, :], in_=a_words[g][:])
@@ -139,8 +138,8 @@ def tile_slstmcell_pb_kernel(tc, x, h_prev, c, n, W_o, b_o, U_o, out):
                     out=ratio_gpsimd[j - VECTOR_TILES][:], in0=c_sb[:, :, cols], in1=inverse[:, :, cols], op=ALU.mult
                 )
 
-        def matmul_pass(g):
-            for j in range(NJ):
+        def matmul_pass(g, units):
+            for j in units:
                 if g == 0:
                     acc[j] = psum.tile([P, BATCH], F32, name="acc%d" % j, tag="bank%d" % j)
                 nc.tensor.matmul_mx(
@@ -183,8 +182,8 @@ def tile_slstmcell_pb_kernel(tc, x, h_prev, c, n, W_o, b_o, U_o, out):
             load_rows(act_sb[0], x, 0, 2)
             load_rows(act_sb[0], x, 2, 4)
             load_rows(act_sb[1], h_prev, 0, 2)
-            load_rows(act_sb[1], h_prev, 2, 4)
             load_weights(2)
+            load_rows(act_sb[1], h_prev, 2, 4)
             load_rows(n_sb, n, 2, 3)
             load_weights(3)
             load_rows(n_sb, n, 3, 4)
@@ -192,32 +191,46 @@ def tile_slstmcell_pb_kernel(tc, x, h_prev, c, n, W_o, b_o, U_o, out):
             load_rows(c_sb, c, 2, 4)
 
             nc.scalar.activation(out=warm[:], in_=eps2[:], func=ACT.Abs_reciprocal_sqrt)
+            interleave(nc.vector.tensor_copy, 0, 0, SPLIT)
+            interleave(nc.scalar.copy, 0, SPLIT, FEAT)
             half_reciprocal(0)
             half_reciprocal(1)
-            interleave(nc.vector.tensor_copy, 0, 0, FEAT)
             flip_bias()
             quantise_weights(0)
             interleave(nc.vector.tensor_copy, 1, 0, FEAT)
             halve_bias()
             quantise_weights(1)
-            flip_acts(0)
+            flip_acts(0, 0)
+            flip_acts(0, 1)
+            unload_acts(nc.scalar.copy, 0, 0)
+            unload_acts(nc.scalar.copy, 0, 1)
+            unload_acts(nc.scalar.copy, 1, 0)
+            unload_acts(nc.vector.tensor_copy, 1, 1)
             quantise_acts(0)
+            interleave(nc.vector.tensor_copy, 2, 0, SPLIT)
+            interleave(nc.scalar.copy, 2, SPLIT, FEAT)
             quantise_acts(1)
-            interleave(nc.vector.tensor_copy, 2, 0, FEAT)
-            flip_acts(1)
-            half_reciprocal(2)
             quantise_weights(2)
-            interleave(nc.vector.tensor_copy, 3, 0, FEAT - SCALAR_COLS)
-            interleave(nc.scalar.copy, 3, FEAT - SCALAR_COLS, FEAT)
+            flip_acts(1, 0)
+            matmul_pass(0, range(4))
+            flip_acts(1, 1)
+            for pair in range(NB // 2):
+                for g in (2, 3):
+                    unload_acts(nc.scalar.copy, g, pair)
             quantise_acts(2)
+            interleave(nc.vector.tensor_copy, 3, 0, FEAT)
             quantise_acts(3)
             quantise_weights(3)
+            half_reciprocal(2)
             half_reciprocal(3)
             for b in range(NB):
                 vector_ratio(b)
             gpsimd_ratios()
-            for g in range(PASSES):
-                matmul_pass(g)
+            matmul_pass(1, range(4))
+            for g in range(2):
+                matmul_pass(g, range(4, NJ))
+            for g in (2, 3):
+                matmul_pass(g, range(NJ))
             for j in range(NJ):
                 gate_of(j)
                 turn_gate(j)

@@ -100,9 +100,9 @@ def tile_slstmcell_pb_kernel(tc, x, h_prev, c, n, W_o, b_o, U_o, out):
                             bank[:, u, i * P : (i + 1) * P], words[:, first + u : first + K_PASS // 2 : 2], ident[:]
                         )
 
-        def unload_acts(copy, g, pair):
+        def unload_acts(g, pair):
             dst = a_words[g][:].bitcast(F32).rearrange("p (r u) -> p r u", u=2)
-            copy(
+            nc.scalar.copy(
                 out=dst[:, 2 * P * pair : 2 * P * (pair + 1), :],
                 in_=flipped[(g, pair)][:].rearrange("p u r -> p r u"),
             )
@@ -117,17 +117,18 @@ def tile_slstmcell_pb_kernel(tc, x, h_prev, c, n, W_o, b_o, U_o, out):
         def halve_bias():
             nc.vector.tensor_scalar_mul(out=bias_half[:], in0=bias_ps[:, 0:NJ], scalar1=0.5)
 
-        def half_reciprocal(b):
-            row = inverse[:, b, :]
-            nc.scalar.activation(
-                out=row, in_=n_sb[:, b, :], func=ACT.Abs_reciprocal_sqrt, bias=eps2[:, 0:1], scale=2.0
-            )
-            nc.scalar.activation(out=row, in_=row, func=ACT.Square)
+        def half_reciprocals(rows):
+            for b in rows:
+                nc.scalar.activation(
+                    out=inverse[:, b, :], in_=n_sb[:, b, :], func=ACT.Abs_reciprocal_sqrt, bias=eps2[:, 0:1], scale=2.0
+                )
+            for b in rows:
+                nc.scalar.activation(out=inverse[:, b, :], in_=inverse[:, b, :], func=ACT.Square)
 
-        def vector_ratio(b):
+        def vector_ratio(lo, hi):
             cols = slice(0, VECTOR_TILES * P)
             nc.vector.tensor_tensor(
-                out=ratio_vector[:, b, :], in0=c_sb[:, b, cols], in1=inverse[:, b, cols], op=ALU.mult
+                out=ratio_vector[:, lo:hi, :], in0=c_sb[:, lo:hi, cols], in1=inverse[:, lo:hi, cols], op=ALU.mult
             )
 
         def gpsimd_ratios():
@@ -193,8 +194,7 @@ def tile_slstmcell_pb_kernel(tc, x, h_prev, c, n, W_o, b_o, U_o, out):
             nc.scalar.activation(out=warm[:], in_=eps2[:], func=ACT.Abs_reciprocal_sqrt)
             interleave(nc.vector.tensor_copy, 0, 0, SPLIT)
             interleave(nc.scalar.copy, 0, SPLIT, FEAT)
-            half_reciprocal(0)
-            half_reciprocal(1)
+            half_reciprocals((0, 1))
             flip_bias()
             quantise_weights(0)
             interleave(nc.vector.tensor_copy, 1, 0, FEAT)
@@ -202,29 +202,29 @@ def tile_slstmcell_pb_kernel(tc, x, h_prev, c, n, W_o, b_o, U_o, out):
             quantise_weights(1)
             flip_acts(0, 0)
             flip_acts(0, 1)
-            unload_acts(nc.scalar.copy, 0, 0)
-            unload_acts(nc.scalar.copy, 0, 1)
-            unload_acts(nc.scalar.copy, 1, 0)
-            unload_acts(nc.vector.tensor_copy, 1, 1)
+            unload_acts(0, 0)
+            unload_acts(0, 1)
+            unload_acts(1, 0)
+            unload_acts(1, 1)
             quantise_acts(0)
+            flip_acts(1, 0)
+            unload_acts(2, 0)
+            unload_acts(3, 0)
             interleave(nc.vector.tensor_copy, 2, 0, SPLIT)
             interleave(nc.scalar.copy, 2, SPLIT, FEAT)
             quantise_acts(1)
             quantise_weights(2)
-            flip_acts(1, 0)
             matmul_pass(0, range(4))
             flip_acts(1, 1)
-            for pair in range(NB // 2):
-                for g in (2, 3):
-                    unload_acts(nc.scalar.copy, g, pair)
+            unload_acts(2, 1)
+            unload_acts(3, 1)
             quantise_acts(2)
             interleave(nc.vector.tensor_copy, 3, 0, FEAT)
             quantise_acts(3)
             quantise_weights(3)
-            half_reciprocal(2)
-            half_reciprocal(3)
-            for b in range(NB):
-                vector_ratio(b)
+            half_reciprocals((2, 3))
+            vector_ratio(0, 2)
+            vector_ratio(2, 4)
             gpsimd_ratios()
             matmul_pass(1, range(4))
             for g in range(2):

@@ -21,7 +21,8 @@ PASSES = 2 * FEAT // K_PASS
 EPS = 1e-6
 
 SPLIT = 3 * FEAT // 4
-VECTOR_TILES = 5
+RATIO_GROUPS = ((0, 2), (2, 3), (5, 1), (6, 1), (7, 1))
+VECTOR_GROUPS = 2
 
 FLOPS = 2 * BATCH * FEAT * FEAT * 2
 
@@ -52,8 +53,7 @@ def tile_slstmcell_pb_kernel(tc, x, h_prev, c, n, W_o, b_o, U_o, out):
         a_codes = keep.tile([P, PASSES, BATCH], U32, name="a_codes", align_bytes=64)
         a_scales = keep.tile([P, PASSES, BATCH], U8, name="a_scales", align_bytes=64)
         inverse = keep.tile([P, NB, FEAT], F32, name="inverse")
-        ratio_vector = keep.tile([P, NB, VECTOR_TILES * P], F32, name="ratio_vector")
-        ratio_gpsimd = [keep.tile([P, NB, P], F32, name="ratio_gpsimd%d" % j) for j in range(VECTOR_TILES, NJ)]
+        ratio = {j: keep.tile([P, NB, width * P], F32, name="ratio%d" % j) for j, width in RATIO_GROUPS}
         mark = keep.tile([P, 1], F32, name="mark")
         gate_t = [keep.tile([P, BATCH], F32, name="gate_t%d" % j) for j in range(NJ)]
         h_sb = keep.tile([P, NB, FEAT], F32, name="h_sb")
@@ -125,19 +125,13 @@ def tile_slstmcell_pb_kernel(tc, x, h_prev, c, n, W_o, b_o, U_o, out):
             for b in rows:
                 nc.scalar.activation(out=inverse[:, b, :], in_=inverse[:, b, :], func=ACT.Square)
 
-        def vector_ratio(lo, hi):
-            cols = slice(0, VECTOR_TILES * P)
-            nc.vector.tensor_tensor(
-                out=ratio_vector[:, lo:hi, :], in0=c_sb[:, lo:hi, cols], in1=inverse[:, lo:hi, cols], op=ALU.mult
-            )
-
-        def gpsimd_ratios():
-            nc.gpsimd.tensor_copy(out=mark[:], in_=ratio_vector[:, NB - 1, VECTOR_TILES * P - 1 : VECTOR_TILES * P])
-            for j in range(VECTOR_TILES, NJ):
-                cols = slice(j * P, (j + 1) * P)
-                nc.gpsimd.tensor_tensor(
-                    out=ratio_gpsimd[j - VECTOR_TILES][:], in0=c_sb[:, :, cols], in1=inverse[:, :, cols], op=ALU.mult
-                )
+        def make_ratios():
+            for i, (j, width) in enumerate(RATIO_GROUPS):
+                engine = nc.vector if i < VECTOR_GROUPS else nc.gpsimd
+                if i == VECTOR_GROUPS:
+                    nc.gpsimd.tensor_copy(out=mark[:], in_=ratio[0][:, NB - 1, 0:1])
+                cols = slice(j * P, (j + width) * P)
+                engine.tensor_tensor(out=ratio[j][:], in0=c_sb[:, :, cols], in1=inverse[:, :, cols], op=ALU.mult)
 
         def matmul_pass(g, units):
             for j in units:
@@ -163,12 +157,10 @@ def tile_slstmcell_pb_kernel(tc, x, h_prev, c, n, W_o, b_o, U_o, out):
 
         def product(j):
             cols = slice(j * P, (j + 1) * P)
-            if j < VECTOR_TILES:
-                ratio = ratio_vector[:, :, cols]
-            else:
-                ratio = ratio_gpsimd[j - VECTOR_TILES][:]
+            first = max(start for start, width in RATIO_GROUPS if start <= j)
+            columns = ratio[first][:, :, (j - first) * P : (j - first + 1) * P]
             nc.vector.scalar_tensor_tensor(
-                out=h_sb[:, :, cols], in0=gate[j][:], scalar=1.0, in1=ratio, op0=ALU.add, op1=ALU.mult
+                out=h_sb[:, :, cols], in0=gate[j][:], scalar=1.0, in1=columns, op0=ALU.add, op1=ALU.mult
             )
 
         def store(j0, j1):
@@ -223,9 +215,7 @@ def tile_slstmcell_pb_kernel(tc, x, h_prev, c, n, W_o, b_o, U_o, out):
             quantise_acts(3)
             quantise_weights(3)
             half_reciprocals((2, 3))
-            vector_ratio(0, 2)
-            vector_ratio(2, 4)
-            gpsimd_ratios()
+            make_ratios()
             matmul_pass(1, range(4))
             for g in range(2):
                 matmul_pass(g, range(4, NJ))

from contextlib import ExitStack

import concourse.masks as masks
import concourse.mybir as mybir

F32 = mybir.dt.float32
BF16 = mybir.dt.bfloat16
U32 = mybir.dt.uint32
U8 = mybir.dt.uint8
FP8X4 = mybir.dt.float8_e4m3fn_x4
ACT = mybir.ActivationFunctionType
ALU = mybir.AluOpType

P = 128
BATCH = 512
FEAT = 1024
NB = BATCH // P
NJ = FEAT // P
K_PASS = 4 * P
PASSES = 2 * FEAT // K_PASS
EPS = 1e-6

SPLIT = 3 * FEAT // 4
RATIO_GROUPS = ((0, 2), (2, 3), (5, 1), (6, 1), (7, 1))
VECTOR_GROUPS = 2

FLOPS = 2 * BATCH * FEAT * FEAT * 2


def tile_slstmcell_pb_kernel(tc, x, h_prev, c, n, W_o, b_o, U_o, out):
    nc = tc.nc
    with ExitStack() as ctx:
        keep = ctx.enter_context(tc.tile_pool(name="keep", bufs=1))
        psum = ctx.enter_context(tc.psum_pool(name="psum", bufs=1))

        ident = keep.tile([P, P], F32, name="ident")
        masks.make_identity(nc, ident[:])
        eps2 = keep.tile([P, 1], F32, name="eps2")
        nc.vector.memset(eps2[:], 2.0 * EPS)
        bias_rows = keep.tile([P, P], BF16, name="bias_rows")
        nc.vector.memset(bias_rows[:], 0.0)

        acts = [x, h_prev]
        weights = [W_o, U_o]
        act_sb = [keep.tile([P, NB, FEAT], BF16, name="act_sb%d" % o) for o in range(2)]
        n_sb = keep.tile([P, NB, FEAT], BF16, name="n_sb")
        c_sb = keep.tile([P, NB, FEAT], BF16, name="c_sb")
        w_rows = [keep.tile([P, 4, FEAT], BF16, name="w_rows%d" % g) for g in range(PASSES)]
        w_words = [keep.tile([P, FEAT, 4], BF16, name="w_words%d" % g, align_bytes=64) for g in range(PASSES)]
        w_codes = keep.tile([P, PASSES, FEAT], U32, name="w_codes", align_bytes=64)
        w_scales = keep.tile([P, PASSES, FEAT], U8, name="w_scales", align_bytes=64)
        a_words = [keep.tile([P, BATCH * 4], BF16, name="a_words%d" % g, align_bytes=64) for g in range(PASSES)]
        a_codes = keep.tile([P, PASSES, BATCH], U32, name="a_codes", align_bytes=64)
        a_scales = keep.tile([P, PASSES, BATCH], U8, name="a_scales", align_bytes=64)
        inverse = keep.tile([P, NB, FEAT], F32, name="inverse")
        ratio = {j: keep.tile([P, NB, width * P], F32, name="ratio%d" % j) for j, width in RATIO_GROUPS}
        mark = keep.tile([P, 1], F32, name="mark")
        gate_t = [keep.tile([P, BATCH], F32, name="gate_t%d" % j) for j in range(NJ)]
        h_sb = keep.tile([P, NB, FEAT], F32, name="h_sb")
        warm = keep.tile([P, 1], F32, name="warm")
        bias_f32 = keep.tile([P, P], F32, name="bias_f32")
        bias_half = keep.tile([P, NJ], F32, name="bias_half")
        bias_ps = psum.tile([P, P], F32, name="bias_ps", tag="bank7")
        flipped = {}
        acc = {}
        gate = {}

        def by_partition(rows):
            return rows.rearrange("(p b) d -> p b d", b=NB)

        def load_rows(dst, src, lo, hi):
            nc.sync.dma_start(out=dst[:, lo:hi, :], in_=by_partition(src)[:, lo:hi, :])

        def load_weights(g):
            rows = weights[g // 2][K_PASS * (g % 2) : K_PASS * (g % 2 + 1), :]
            nc.sync.dma_start(out=w_rows[g][:], in_=rows.rearrange("(p t) w -> p t w", t=4))

        def interleave(copy, g, lo, hi):
            copy(
                out=w_words[g][:, lo:hi, :].rearrange("p (w i) t -> p w t i", i=4),
                in_=w_rows[g][:, :, lo:hi].rearrange("p t (w i) -> p w t i", i=4),
            )

        def quantise_weights(g):
            nc.vector.quantize_mx(
                out=w_codes[:, g, :].bitcast(FP8X4),
                scales=w_scales[:, g, :],
                in_=w_words[g][:].rearrange("p w t -> p (w t)"),
            )

        def flip_acts(o, pair):
            for g in (2 * o, 2 * o + 1):
                bank = psum.tile([P, 2, 2 * P], F32, name="flipped%d_%d" % (g, pair), tag="bank%d" % (2 * g + pair))
                flipped[(g, pair)] = bank
                for u in range(2):
                    for i in range(2):
                        words = act_sb[o][:, 2 * pair + i, :].bitcast(F32)
                        first = (K_PASS // 2) * (g % 2)
                        nc.tensor.transpose(
                            bank[:, u, i * P : (i + 1) * P], words[:, first + u : first + K_PASS // 2 : 2], ident[:]
                        )

        def unload_acts(g, pair):
            dst = a_words[g][:].bitcast(F32).rearrange("p (r u) -> p r u", u=2)
            nc.scalar.copy(
                out=dst[:, 2 * P * pair : 2 * P * (pair + 1), :],
                in_=flipped[(g, pair)][:].rearrange("p u r -> p r u"),
            )

        def quantise_acts(g):
            nc.vector.quantize_mx(out=a_codes[:, g, :].bitcast(FP8X4), scales=a_scales[:, g, :], in_=a_words[g][:])

        def flip_bias():
            nc.vector.tensor_copy(out=bias_f32[:], in_=bias_rows[:])
            nc.tensor.transpose(bias_ps[:], bias_f32[:], ident[:])

        def halve_bias():
            nc.vector.tensor_scalar_mul(out=bias_half[:], in0=bias_ps[:, 0:NJ], scalar1=0.5)

        def half_reciprocals(rows):
            for b in rows:
                nc.scalar.activation(
                    out=inverse[:, b, :], in_=n_sb[:, b, :], func=ACT.Abs_reciprocal_sqrt, bias=eps2[:, 0:1], scale=2.0
                )
            for b in rows:
                nc.scalar.activation(out=inverse[:, b, :], in_=inverse[:, b, :], func=ACT.Square)

        def make_ratios():
            for i, (j, width) in enumerate(RATIO_GROUPS):
                engine = nc.vector if i < VECTOR_GROUPS else nc.gpsimd
                if i == VECTOR_GROUPS:
                    nc.gpsimd.tensor_copy(out=mark[:], in_=ratio[0][:, NB - 1, 0:1])
                cols = slice(j * P, (j + width) * P)
                engine.tensor_tensor(out=ratio[j][:], in0=c_sb[:, :, cols], in1=inverse[:, :, cols], op=ALU.mult)

        def matmul_pass(g, units):
            for j in units:
                if g == 0:
                    acc[j] = psum.tile([P, BATCH], F32, name="acc%d" % j, tag="bank%d" % j)
                nc.tensor.matmul_mx(
                    out=acc[j][:],
                    lhsT=w_codes[:, g, j * P : (j + 1) * P].bitcast(FP8X4),
                    lhsT_scale=w_scales[:, g, j * P : (j + 1) * P],
                    rhs=a_codes[:, g, :].bitcast(FP8X4),
                    rhs_scale=a_scales[:, g, :],
                    start=(g == 0),
                    stop=(g == PASSES - 1),
                )

        def gate_of(j):
            nc.scalar.activation(out=gate_t[j][:], in_=acc[j][:], func=ACT.Tanh, bias=bias_half[:, j : j + 1], scale=0.5)

        def turn_gate(j):
            gate[j] = psum.tile([P, NB, P], F32, name="gate%d" % j, tag="bank%d" % j)
            for b in range(NB):
                nc.tensor.transpose(gate[j][:, b, :], gate_t[j][:, b * P : (b + 1) * P], ident[:])

        def product(j):
            cols = slice(j * P, (j + 1) * P)
            first = max(start for start, width in RATIO_GROUPS if start <= j)
            columns = ratio[first][:, :, (j - first) * P : (j - first + 1) * P]
            nc.vector.scalar_tensor_tensor(
                out=h_sb[:, :, cols], in0=gate[j][:], scalar=1.0, in1=columns, op0=ALU.add, op1=ALU.mult
            )

        def store(j0, j1):
            cols = slice(j0 * P, j1 * P)
            nc.sync.dma_start(out=by_partition(out)[:, :, cols], in_=h_sb[:, :, cols])

        with tc.manual_schedule():
            load_weights(0)
            load_rows(n_sb, n, 0, 2)
            nc.sync.dma_start(out=bias_rows[0:NJ, :], in_=b_o.rearrange("(j p) -> j p", p=P))
            load_weights(1)
            load_rows(act_sb[0], x, 0, 2)
            load_rows(act_sb[0], x, 2, 4)
            load_rows(act_sb[1], h_prev, 0, 2)
            load_weights(2)
            load_rows(act_sb[1], h_prev, 2, 4)
            load_rows(n_sb, n, 2, 3)
            load_weights(3)
            load_rows(n_sb, n, 3, 4)
            load_rows(c_sb, c, 0, 2)
            load_rows(c_sb, c, 2, 4)

            nc.scalar.activation(out=warm[:], in_=eps2[:], func=ACT.Abs_reciprocal_sqrt)
            interleave(nc.vector.tensor_copy, 0, 0, SPLIT)
            interleave(nc.scalar.copy, 0, SPLIT, FEAT)
            half_reciprocals((0, 1))
            flip_bias()
            quantise_weights(0)
            interleave(nc.vector.tensor_copy, 1, 0, FEAT)
            halve_bias()
            quantise_weights(1)
            flip_acts(0, 0)
            flip_acts(0, 1)
            unload_acts(0, 0)
            unload_acts(0, 1)
            unload_acts(1, 0)
            unload_acts(1, 1)
            quantise_acts(0)
            flip_acts(1, 0)
            unload_acts(2, 0)
            unload_acts(3, 0)
            interleave(nc.vector.tensor_copy, 2, 0, SPLIT)
            interleave(nc.scalar.copy, 2, SPLIT, FEAT)
            quantise_acts(1)
            quantise_weights(2)
            matmul_pass(0, range(4))
            flip_acts(1, 1)
            unload_acts(2, 1)
            unload_acts(3, 1)
            quantise_acts(2)
            interleave(nc.vector.tensor_copy, 3, 0, FEAT)
            quantise_acts(3)
            quantise_weights(3)
            half_reciprocals((2, 3))
            make_ratios()
            matmul_pass(1, range(4))
            for g in range(2):
                matmul_pass(g, range(4, NJ))
            for g in (2, 3):
                matmul_pass(g, range(NJ))
            for j in range(NJ):
                gate_of(j)
                turn_gate(j)
                product(j)
                if j % 2 == 1:
                    store(j - 1, j + 1)
